import numpy as np
import ml_dtypes

BF16 = ml_dtypes.bfloat16


def bf(x):
    return np.asarray(x, np.float32).astype(BF16)


def f32(x):
    return np.asarray(x, np.float32)


def f64(x):
    return np.asarray(x).astype(np.float64)


def striped(idx):
    return np.tile(idx.reshape(-1, 16).T, (8, 1))


C, S, N, K = 512, 256, 128, 128
XS, YS = 0.5, 2.0


def setup_inputs():
    return {"x": f32(XS * np.random.standard_normal((C, S))), "y": f32(YS * np.random.standard_normal((N, K))), "offs": striped(np.random.permutation(S)[:N])}


def reference(x, y, offs):
    idx = offs[:16].T.reshape(-1)
    xp = f64(x)[:, idx]
    nrm = np.sum(xp * xp, axis=0)
    sq = np.maximum(nrm[:, None] + nrm[None, :] - 2.0 * (xp.T @ xp), 0.0)
    d = np.sqrt(sq)
    e = np.exp(np.max(d) - d) * (1.0 - np.eye(idx.size))
    p = e / np.sum(e, axis=1, keepdims=True)
    return (p @ f64(y)).T

@@ -1,0 +1,95 @@
+import concourse.mybir as mybir
+from concourse.masks import make_identity
+
+F32 = mybir.dt.float32
+BF16 = mybir.dt.bfloat16
+U16 = mybir.dt.uint16
+ALU = mybir.AluOpType
+ACT = mybir.ActivationFunctionType
+
+P = 128
+C, S, N, K = 512, 256, 128, 128
+BLOCKS = C // P
+
+FLOPS = 2 * N * N * C + 2 * N * N * K
+
+SMALL = 2.0 ** -100
+BIG = 2.0 ** 100
+
+
+def tile_nona_nn_kernel(tc, x, y, offs, out):
+    nc = tc.nc
+    with (
+        tc.tile_pool(name="held", bufs=1) as held,
+        tc.psum_pool(name="psum", bufs=1) as psum,
+    ):
+        offsets = held.tile([P, N // 16], U16, name="offsets")
+        nc.sync.dma_start(offsets[:], offs)
+        x_blocks = x.rearrange("(b p) s -> b p s", p=P)
+        windows = [held.tile([P, S], F32, name=f"window{b}") for b in range(BLOCKS)]
+        for b in range(BLOCKS):
+            queue = nc.sync if b % 2 == 0 else nc.scalar
+            queue.dma_start(windows[b][:], x_blocks[b])
+        y_f32 = held.tile([N, K], F32, name="y_f32")
+        nc.sync.dma_start(y_f32[:], y)
+
+        identity = held.tile([P, P], BF16, name="identity")
+        make_identity(nc, identity[:])
+        diagonal = held.tile([P, P], BF16, name="diagonal")
+        nc.gpsimd.memset(diagonal[:], 0.0)
+        nc.gpsimd.affine_select(
+            out=diagonal[:],
+            in_=diagonal[:],
+            compare_op=ALU.not_equal,
+            fill=-BIG / 2,
+            base=0,
+            pattern=[[-1, P]],
+            channel_multiplier=1,
+        )
+        minus_half = held.tile([P, P], BF16, name="minus_half")
+        nc.vector.memset(minus_half[:], -0.5)
+        y_bf = held.tile([N, K], BF16, name="y_bf")
+        nc.gpsimd.tensor_copy(y_bf[:], y_f32[:])
+
+        half = psum.tile([N, N], F32, name="half")
+        nc.tensor.matmul(half[:], identity[:], diagonal[:], start=True, stop=False)
+        for b in range(BLOCKS):
+            picked = held.tile([P, N], F32, name=f"picked{b}")
+            nc.scalar.activation(picked[:], windows[b][:].indirect(offsets[:]), ACT.Copy)
+            picked_bf = held.tile([P, N], BF16, name=f"picked_bf{b}")
+            nc.vector.tensor_copy(picked_bf[:], picked[:])
+            squares_bf = held.tile([P, N], BF16, name=f"squares_bf{b}")
+            nc.vector.tensor_tensor(squares_bf[:], picked[:], picked[:], ALU.mult)
+            nc.tensor.matmul(half[:], picked_bf[:], picked_bf[:], start=False, stop=False)
+            nc.tensor.matmul(half[:], minus_half[:], squares_bf[:], start=False, stop=False)
+            nc.tensor.matmul(
+                half[:], squares_bf[:], minus_half[:], start=False, stop=(b == BLOCKS - 1)
+            )
+
+        squared = held.tile([N, N], F32, name="squared")
+        nc.vector.tensor_scalar(squared[:], half[:], -2.0, SMALL, ALU.mult, ALU.max)
+        dist = held.tile([N, N], F32, name="dist")
+        nc.scalar.activation(dist[:], squared[:], ACT.Sqrt)
+
+        nearest = held.tile([N, 1], F32, name="nearest")
+        nc.vector.tensor_reduce(nearest[:], dist[:], mybir.AxisListType.X, ALU.min)
+        grown = held.tile([N, N], F32, name="grown")
+        total = held.tile([N, 1], F32, name="total")
+        nc.scalar.activation(
+            grown[:], dist[:], ACT.Exp, bias=nearest[:], scale=-1.0, accum_out=total[:]
+        )
+        inverse = held.tile([N, 1], F32, name="inverse")
+        nc.vector.reciprocal(inverse[:], total[:])
+        weights = held.tile([N, N], BF16, name="weights")
+        nc.vector.tensor_scalar(weights[:], grown[:], inverse[:], None, ALU.mult)
+
+        weights_t_ps = psum.tile([N, N], BF16, name="weights_t_ps")
+        nc.tensor.transpose(weights_t_ps[:], weights[:], identity[:])
+        weights_t = held.tile([N, N], BF16, name="weights_t")
+        nc.vector.tensor_copy(weights_t[:], weights_t_ps[:])
+
+        mixed = psum.tile([K, N], F32, name="mixed")
+        nc.tensor.matmul(mixed[:], y_bf[:], weights_t[:], start=True, stop=True)
+        result = held.tile([K, N], F32, name="result")
+        nc.vector.tensor_copy(result[:], mixed[:])
+        nc.sync.dma_start(out, result[:])

@@ -33,6 +33,10 @@ def tile_nona_nn_kernel(tc, x, y, offs, out):
         y_f32 = held.tile([N, K], F32, name="y_f32")
         nc.sync.dma_start(y_f32[:], y)
 
+        warm = held.tile([P, 1], F32, name="warm")
+        nc.gpsimd.memset(warm[:], 1.0)
+        nc.scalar.activation(warm[:], warm[:], ACT.Sqrt)
+
         identity = held.tile([P, P], BF16, name="identity")
         make_identity(nc, identity[:])
         diagonal = held.tile([P, P], BF16, name="diagonal")

@@ -28,8 +28,7 @@ def tile_nona_nn_kernel(tc, x, y, offs, out):
         x_blocks = x.rearrange("(b p) s -> b p s", p=P)
         windows = [held.tile([P, S], F32, name=f"window{b}") for b in range(BLOCKS)]
         for b in range(BLOCKS):
-            queue = nc.sync if b % 2 == 0 else nc.scalar
-            queue.dma_start(windows[b][:], x_blocks[b])
+            nc.sync.dma_start(windows[b][:], x_blocks[b])
         y_f32 = held.tile([N, K], F32, name="y_f32")
         nc.sync.dma_start(y_f32[:], y)
 

@@ -11,6 +11,9 @@ P = 128
 C, S, N, K = 512, 256, 128, 128
 BLOCKS = C // P
 
+BANK = 512
+WARM_UPS = 4
+
 FLOPS = 2 * N * N * C + 2 * N * N * K
 
 SMALL = 2.0 ** -100
@@ -53,6 +56,12 @@ def tile_nona_nn_kernel(tc, x, y, offs, out):
         nc.vector.memset(minus_half[:], -0.5)
         y_bf = held.tile([N, K], BF16, name="y_bf")
         nc.gpsimd.tensor_copy(y_bf[:], y_f32[:])
+
+        filler = held.tile([P, BANK], BF16, name="filler")
+        nc.vector.memset(filler[:], 0.0)
+        unused = psum.tile([P, BANK], F32, name="unused")
+        for warm_up in range(WARM_UPS):
+            nc.tensor.matmul(unused[:], minus_half[:], filler[:], start=True, stop=True)
 
         half = psum.tile([N, N], F32, name="half")
         nc.tensor.matmul(half[:], identity[:], diagonal[:], start=True, stop=False)

@@ -16,8 +16,8 @@ WARM_UPS = 4
 
 FLOPS = 2 * N * N * C + 2 * N * N * K
 
-SMALL = 2.0 ** -100
-BIG = 2.0 ** 100
+SMALL = 2.0 ** -80
+BIG = 2.0 ** 96
 
 
 def tile_nona_nn_kernel(tc, x, y, offs, out):
@@ -37,7 +37,7 @@ def tile_nona_nn_kernel(tc, x, y, offs, out):
 
         warm = held.tile([P, 1], F32, name="warm")
         nc.gpsimd.memset(warm[:], 1.0)
-        nc.scalar.activation(warm[:], warm[:], ACT.Sqrt)
+        nc.scalar.activation(warm[:], warm[:], ACT.Abs_reciprocal_sqrt)
 
         identity = held.tile([P, P], BF16, name="identity")
         make_identity(nc, identity[:])
@@ -52,6 +52,8 @@ def tile_nona_nn_kernel(tc, x, y, offs, out):
             pattern=[[-1, P]],
             channel_multiplier=1,
         )
+        identity_f32 = held.tile([P, P], F32, name="identity_f32")
+        make_identity(nc, identity_f32[:])
         minus_half = held.tile([P, P], BF16, name="minus_half")
         nc.vector.memset(minus_half[:], -0.5)
         y_bf = held.tile([N, K], BF16, name="y_bf")
@@ -78,30 +80,36 @@ def tile_nona_nn_kernel(tc, x, y, offs, out):
                 half[:], squares_bf[:], minus_half[:], start=False, stop=(b == BLOCKS - 1)
             )
 
-        squared = held.tile([N, N], F32, name="squared")
-        nc.vector.tensor_scalar(squared[:], half[:], -2.0, SMALL, ALU.mult, ALU.max)
-        dist = held.tile([N, N], F32, name="dist")
-        nc.scalar.activation(dist[:], squared[:], ACT.Sqrt)
+        root = held.tile([N, N], F32, name="root")
+        nc.scalar.activation(root[:], half[:], ACT.Abs_reciprocal_sqrt, bias=-SMALL, scale=0.5)
+        signed = held.tile([N, N], F32, name="signed")
+        nc.vector.scalar_tensor_tensor(signed[:], half[:], -1.0, root[:], ALU.mult, ALU.mult)
 
+        dist = held.tile([N, N], F32, name="dist")
         nearest = held.tile([N, 1], F32, name="nearest")
-        nc.vector.tensor_reduce(nearest[:], dist[:], mybir.AxisListType.X, ALU.min)
-        grown = held.tile([N, N], F32, name="grown")
+        nc.vector.tensor_scalar(dist[:], signed[:], 0.0, None, ALU.max, ALU.min, accum_out=nearest[:])
+        weights = held.tile([N, N], BF16, name="weights")
         total = held.tile([N, 1], F32, name="total")
         nc.scalar.activation(
-            grown[:], dist[:], ACT.Exp, bias=nearest[:], scale=-1.0, accum_out=total[:]
+            weights[:], dist[:], ACT.Exp, bias=nearest[:], scale=-1.0, accum_out=total[:]
         )
-        inverse = held.tile([N, 1], F32, name="inverse")
-        nc.vector.reciprocal(inverse[:], total[:])
-        weights = held.tile([N, N], BF16, name="weights")
-        nc.vector.tensor_scalar(weights[:], grown[:], inverse[:], None, ALU.mult)
 
         weights_t_ps = psum.tile([N, N], BF16, name="weights_t_ps")
         nc.tensor.transpose(weights_t_ps[:], weights[:], identity[:])
         weights_t = held.tile([N, N], BF16, name="weights_t")
         nc.vector.tensor_copy(weights_t[:], weights_t_ps[:])
 
+        inverse = held.tile([N, 1], F32, name="inverse")
+        nc.vector.reciprocal(inverse[:], total[:])
+        spread_ps = psum.tile([K, N], F32, name="spread_ps")
+        nc.tensor.matmul(
+            spread_ps[:], inverse[:].to_broadcast([N, K]), identity_f32[:], start=True, stop=True
+        )
+        spread = held.tile([K, N], F32, name="spread")
+        nc.scalar.copy(spread[:], spread_ps[:])
+
         mixed = psum.tile([K, N], F32, name="mixed")
         nc.tensor.matmul(mixed[:], y_bf[:], weights_t[:], start=True, stop=True)
         result = held.tile([K, N], F32, name="result")
-        nc.vector.tensor_copy(result[:], mixed[:])
+        nc.vector.tensor_tensor(result[:], mixed[:], spread[:], ALU.mult)
         nc.sync.dma_start(out, result[:])

@@ -102,9 +102,7 @@ def tile_nona_nn_kernel(tc, x, y, offs, out):
         inverse = held.tile([N, 1], F32, name="inverse")
         nc.vector.reciprocal(inverse[:], total[:])
         spread_ps = psum.tile([K, N], F32, name="spread_ps")
-        nc.tensor.matmul(
-            spread_ps[:], inverse[:].to_broadcast([N, K]), identity_f32[:], start=True, stop=True
-        )
+        nc.tensor.transpose(spread_ps[:], inverse[:].to_broadcast([N, K]), identity_f32[:])
         spread = held.tile([K, N], F32, name="spread")
         nc.scalar.copy(spread[:], spread_ps[:])
 

@@ -104,7 +104,7 @@ def tile_nona_nn_kernel(tc, x, y, offs, out):
         spread_ps = psum.tile([K, N], F32, name="spread_ps")
         nc.tensor.transpose(spread_ps[:], inverse[:].to_broadcast([N, K]), identity_f32[:])
         spread = held.tile([K, N], F32, name="spread")
-        nc.scalar.copy(spread[:], spread_ps[:])
+        nc.vector.tensor_copy(spread[:], spread_ps[:])
 
         mixed = psum.tile([K, N], F32, name="mixed")
         nc.tensor.matmul(mixed[:], y_bf[:], weights_t[:], start=True, stop=True)

@@ -13,6 +13,7 @@ BLOCKS = C // P
 
 BANK = 512
 WARM_UPS = 4
+KEEP_UPS = 2
 
 FLOPS = 2 * N * N * C + 2 * N * N * K
 
@@ -61,6 +62,8 @@ def tile_nona_nn_kernel(tc, x, y, offs, out):
 
         filler = held.tile([P, BANK], BF16, name="filler")
         nc.vector.memset(filler[:], 0.0)
+        filler_f32 = held.tile([P, BANK // 2], F32, name="filler_f32")
+        nc.vector.memset(filler_f32[:], 0.0)
         unused = psum.tile([P, BANK], F32, name="unused")
         for warm_up in range(WARM_UPS):
             nc.tensor.matmul(unused[:], minus_half[:], filler[:], start=True, stop=True)
@@ -82,6 +85,8 @@ def tile_nona_nn_kernel(tc, x, y, offs, out):
 
         root = held.tile([N, N], F32, name="root")
         nc.scalar.activation(root[:], half[:], ACT.Abs_reciprocal_sqrt, bias=-SMALL, scale=0.5)
+        for keep_up in range(KEEP_UPS):
+            nc.tensor.matmul(unused[:, 0 : BANK // 2], root[:], filler_f32[:], start=True, stop=True)
         signed = held.tile([N, N], F32, name="signed")
         nc.vector.scalar_tensor_tensor(signed[:], half[:], -1.0, root[:], ALU.mult, ALU.mult)
 
@@ -104,7 +109,7 @@ def tile_nona_nn_kernel(tc, x, y, offs, out):
         spread_ps = psum.tile([K, N], F32, name="spread_ps")
         nc.tensor.transpose(spread_ps[:], inverse[:].to_broadcast([N, K]), identity_f32[:])
         spread = held.tile([K, N], F32, name="spread")
-        nc.vector.tensor_copy(spread[:], spread_ps[:])
+        nc.scalar.copy(spread[:], spread_ps[:])
 
         mixed = psum.tile([K, N], F32, name="mixed")
         nc.tensor.matmul(mixed[:], y_bf[:], weights_t[:], start=True, stop=True)

@@ -28,10 +28,11 @@ def tile_nona_nn_kernel(tc, x, y, offs, out):
         tc.psum_pool(name="psum", bufs=1) as psum,
     ):
         offsets = held.tile([P, N // 16], U16, name="offsets")
-        nc.sync.dma_start(offsets[:], offs)
         x_blocks = x.rearrange("(b p) s -> b p s", p=P)
         windows = [held.tile([P, S], F32, name=f"window{b}") for b in range(BLOCKS)]
-        for b in range(BLOCKS):
+        nc.sync.dma_start(windows[0][:], x_blocks[0])
+        nc.sync.dma_start(offsets[:], offs)
+        for b in range(1, BLOCKS):
             nc.sync.dma_start(windows[b][:], x_blocks[b])
         y_f32 = held.tile([N, K], F32, name="y_f32")
         nc.sync.dma_start(y_f32[:], y)

@@ -77,7 +77,10 @@ def tile_nona_nn_kernel(tc, x, y, offs, out):
             picked_bf = held.tile([P, N], BF16, name=f"picked_bf{b}")
             nc.vector.tensor_copy(picked_bf[:], picked[:])
             squares_bf = held.tile([P, N], BF16, name=f"squares_bf{b}")
-            nc.vector.tensor_tensor(squares_bf[:], picked[:], picked[:], ALU.mult)
+            if b < BLOCKS - 1:
+                nc.vector.tensor_tensor(squares_bf[:], picked[:], picked[:], ALU.mult)
+            else:
+                nc.scalar.activation(squares_bf[:], picked[:], ACT.Square)
             nc.tensor.matmul(half[:], picked_bf[:], picked_bf[:], start=False, stop=False)
             nc.tensor.matmul(half[:], minus_half[:], squares_bf[:], start=False, stop=False)
             nc.tensor.matmul(

@@ -55,11 +55,9 @@ def tile_nona_nn_kernel(tc, x, y, offs, out):
             channel_multiplier=1,
         )
         identity_f32 = held.tile([P, P], F32, name="identity_f32")
-        make_identity(nc, identity_f32[:])
+        nc.vector.tensor_copy(identity_f32[:], identity[:])
         minus_half = held.tile([P, P], BF16, name="minus_half")
         nc.vector.memset(minus_half[:], -0.5)
-        y_bf = held.tile([N, K], BF16, name="y_bf")
-        nc.gpsimd.tensor_copy(y_bf[:], y_f32[:])
 
         filler = held.tile([P, BANK], BF16, name="filler")
         nc.vector.memset(filler[:], 0.0)
@@ -86,6 +84,9 @@ def tile_nona_nn_kernel(tc, x, y, offs, out):
             nc.tensor.matmul(
                 half[:], squares_bf[:], minus_half[:], start=False, stop=(b == BLOCKS - 1)
             )
+
+        y_bf = held.tile([N, K], BF16, name="y_bf")
+        nc.scalar.copy(y_bf[:], y_f32[:])
 
         root = held.tile([N, N], F32, name="root")
         nc.scalar.activation(root[:], half[:], ACT.Abs_reciprocal_sqrt, bias=-SMALL, scale=0.5)

@@ -13,7 +13,6 @@ BLOCKS = C // P
 
 BANK = 512
 WARM_UPS = 4
-KEEP_UPS = 2
 
 FLOPS = 2 * N * N * C + 2 * N * N * K
 
@@ -61,8 +60,6 @@ def tile_nona_nn_kernel(tc, x, y, offs, out):
 
         filler = held.tile([P, BANK], BF16, name="filler")
         nc.vector.memset(filler[:], 0.0)
-        filler_f32 = held.tile([P, BANK // 2], F32, name="filler_f32")
-        nc.vector.memset(filler_f32[:], 0.0)
         unused = psum.tile([P, BANK], F32, name="unused")
         for warm_up in range(WARM_UPS):
             nc.tensor.matmul(unused[:], minus_half[:], filler[:], start=True, stop=True)
@@ -90,34 +87,36 @@ def tile_nona_nn_kernel(tc, x, y, offs, out):
 
         root = held.tile([N, N], F32, name="root")
         nc.scalar.activation(root[:], half[:], ACT.Abs_reciprocal_sqrt, bias=-SMALL, scale=0.5)
-        for keep_up in range(KEEP_UPS):
-            nc.tensor.matmul(unused[:, 0 : BANK // 2], root[:], filler_f32[:], start=True, stop=True)
-        signed = held.tile([N, N], F32, name="signed")
-        nc.vector.scalar_tensor_tensor(signed[:], half[:], -1.0, root[:], ALU.mult, ALU.mult)
-
-        dist = held.tile([N, N], F32, name="dist")
-        nearest = held.tile([N, 1], F32, name="nearest")
-        nc.vector.tensor_scalar(dist[:], signed[:], 0.0, None, ALU.max, ALU.min, accum_out=nearest[:])
-        weights = held.tile([N, N], BF16, name="weights")
-        total = held.tile([N, 1], F32, name="total")
-        nc.scalar.activation(
-            weights[:], dist[:], ACT.Exp, bias=nearest[:], scale=-1.0, accum_out=total[:]
+        minus_dist = held.tile([N, N], F32, name="minus_dist")
+        nc.vector.scalar_tensor_tensor(minus_dist[:], half[:], 0.0, root[:], ALU.min, ALU.mult)
+        nearest = held.tile([N, 1], BF16, name="nearest")
+        nc.vector.tensor_reduce(
+            nearest[:], minus_dist[:], axis=mybir.AxisListType.X, op=ALU.max, negate=True
         )
 
-        weights_t_ps = psum.tile([N, N], BF16, name="weights_t_ps")
-        nc.tensor.transpose(weights_t_ps[:], weights[:], identity[:])
+        exponents_t = psum.tile([N, N], F32, name="exponents_t")
+        nc.tensor.matmul(exponents_t[:], identity_f32[:], minus_dist[:], start=True, stop=False)
+        nc.tensor.matmul(
+            exponents_t[:], nearest[:].to_broadcast([N, N]), identity[:], start=False, stop=True
+        )
+
         weights_t = held.tile([N, N], BF16, name="weights_t")
-        nc.vector.tensor_copy(weights_t[:], weights_t_ps[:])
+        nc.scalar.activation(weights_t[:], exponents_t[:], ACT.Exp)
+        total = held.tile([N, 1], F32, name="total")
+        nc.scalar.activation(
+            identity[:], minus_dist[:], ACT.Exp, bias=nearest[:], accum_out=total[:]
+        )
+
+        mixed_ps = psum.tile([K, N], F32, name="mixed_ps")
+        nc.tensor.matmul(mixed_ps[:], y_bf[:], weights_t[:], start=True, stop=True)
 
         inverse = held.tile([N, 1], F32, name="inverse")
         nc.vector.reciprocal(inverse[:], total[:])
         spread_ps = psum.tile([K, N], F32, name="spread_ps")
         nc.tensor.transpose(spread_ps[:], inverse[:].to_broadcast([N, K]), identity_f32[:])
-        spread = held.tile([K, N], F32, name="spread")
-        nc.scalar.copy(spread[:], spread_ps[:])
 
-        mixed = psum.tile([K, N], F32, name="mixed")
-        nc.tensor.matmul(mixed[:], y_bf[:], weights_t[:], start=True, stop=True)
+        mixed = held.tile([K, N], F32, name="mixed")
+        nc.scalar.copy(mixed[:], mixed_ps[:])
         result = held.tile([K, N], F32, name="result")
-        nc.vector.tensor_tensor(result[:], mixed[:], spread[:], ALU.mult)
+        nc.vector.tensor_tensor(result[:], mixed[:], spread_ps[:], ALU.mult)
         nc.sync.dma_start(out, result[:])

@@ -13,6 +13,7 @@ BLOCKS = C // P
 
 BANK = 512
 WARM_UPS = 4
+KEEP_UPS = 2
 
 FLOPS = 2 * N * N * C + 2 * N * N * K
 
@@ -99,6 +100,11 @@ def tile_nona_nn_kernel(tc, x, y, offs, out):
         nc.tensor.matmul(
             exponents_t[:], nearest[:].to_broadcast([N, N]), identity[:], start=False, stop=True
         )
+
+        for keep_up in range(KEEP_UPS):
+            nc.tensor.matmul(
+                unused[:], nearest[:].to_broadcast([N, N]), filler[:], start=True, stop=True
+            )
 
         weights_t = held.tile([N, N], BF16, name="weights_t")
         nc.scalar.activation(weights_t[:], exponents_t[:], ACT.Exp)

@@ -28,7 +28,7 @@ def tile_nona_nn_kernel(tc, x, y, offs, out):
         tc.psum_pool(name="psum", bufs=1) as psum,
     ):
         offsets = held.tile([P, N // 16], U16, name="offsets")
-        x_blocks = x.rearrange("(b p) s -> b p s", p=P)
+        x_blocks = x.rearrange("(p b) s -> b p s", p=P)
         windows = [held.tile([P, S], F32, name=f"window{b}") for b in range(BLOCKS)]
         nc.sync.dma_start(windows[0][:], x_blocks[0])
         nc.sync.dma_start(offsets[:], offs)

@@ -106,15 +106,19 @@ def tile_nona_nn_kernel(tc, x, y, offs, out):
                 unused[:], nearest[:].to_broadcast([N, N]), filler[:], start=True, stop=True
             )
 
-        weights_t = held.tile([N, N], BF16, name="weights_t")
-        nc.scalar.activation(weights_t[:], exponents_t[:], ACT.Exp)
+        weights = held.tile([N, N], BF16, name="weights")
         total = held.tile([N, 1], F32, name="total")
         nc.scalar.activation(
-            identity[:], minus_dist[:], ACT.Exp, bias=nearest[:], accum_out=total[:]
+            weights[:], minus_dist[:], ACT.Exp, bias=nearest[:], accum_out=total[:]
         )
+        weights_t = held.tile([N, N], BF16, name="weights_t")
+        nc.scalar.activation(weights_t[:], exponents_t[:], ACT.Exp)
 
-        mixed_ps = psum.tile([K, N], F32, name="mixed_ps")
-        nc.tensor.matmul(mixed_ps[:], y_bf[:], weights_t[:], start=True, stop=True)
+        HALF = N // 2
+        mixed_low_ps = psum.tile([K, HALF], F32, name="mixed_low_ps")
+        mixed_high_ps = psum.tile([K, HALF], F32, name="mixed_high_ps")
+        nc.tensor.matmul(mixed_low_ps[:], y_bf[:], weights_t[:, 0:HALF], start=True, stop=True)
+        nc.tensor.matmul(mixed_high_ps[:], y_bf[:], weights_t[:, HALF:N], start=True, stop=True)
 
         inverse = held.tile([N, 1], F32, name="inverse")
         nc.vector.reciprocal(inverse[:], total[:])
@@ -122,7 +126,8 @@ def tile_nona_nn_kernel(tc, x, y, offs, out):
         nc.tensor.transpose(spread_ps[:], inverse[:].to_broadcast([N, K]), identity_f32[:])
 
         mixed = held.tile([K, N], F32, name="mixed")
-        nc.scalar.copy(mixed[:], mixed_ps[:])
+        nc.vector.tensor_copy(mixed[:, 0:HALF], mixed_low_ps[:])
+        nc.scalar.copy(mixed[:, HALF:N], mixed_high_ps[:])
         result = held.tile([K, N], F32, name="result")
         nc.vector.tensor_tensor(result[:], mixed[:], spread_ps[:], ALU.mult)
         nc.sync.dma_start(out, result[:])

@@ -28,12 +28,15 @@ def tile_nona_nn_kernel(tc, x, y, offs, out):
         tc.psum_pool(name="psum", bufs=1) as psum,
     ):
         offsets = held.tile([P, N // 16], U16, name="offsets")
-        x_blocks = x.rearrange("(p b) s -> b p s", p=P)
-        windows = [held.tile([P, S], F32, name=f"window{b}") for b in range(BLOCKS)]
-        nc.sync.dma_start(windows[0][:], x_blocks[0])
+        x_rows = x.rearrange("(p b) s -> p (b s)", p=P)
+        first = held.tile([P, S], F32, name="first")
+        second = held.tile([P, S], F32, name="second")
+        last_two = held.tile([P, 2 * S], F32, name="last_two")
+        windows = [first[:], second[:], last_two[:, 0:S], last_two[:, S : 2 * S]]
+        nc.sync.dma_start(first[:], x_rows[:, 0:S])
         nc.sync.dma_start(offsets[:], offs)
-        for b in range(1, BLOCKS):
-            nc.sync.dma_start(windows[b][:], x_blocks[b])
+        nc.sync.dma_start(second[:], x_rows[:, S : 2 * S])
+        nc.sync.dma_start(last_two[:], x_rows[:, 2 * S : 4 * S])
         y_f32 = held.tile([N, K], F32, name="y_f32")
         nc.sync.dma_start(y_f32[:], y)
 
@@ -69,7 +72,7 @@ def tile_nona_nn_kernel(tc, x, y, offs, out):
         nc.tensor.matmul(half[:], identity[:], diagonal[:], start=True, stop=False)
         for b in range(BLOCKS):
             picked = held.tile([P, N], F32, name=f"picked{b}")
-            nc.scalar.activation(picked[:], windows[b][:].indirect(offsets[:]), ACT.Copy)
+            nc.scalar.activation(picked[:], windows[b].indirect(offsets[:]), ACT.Copy)
             picked_bf = held.tile([P, N], BF16, name=f"picked_bf{b}")
             nc.vector.tensor_copy(picked_bf[:], picked[:])
             squares_bf = held.tile([P, N], BF16, name=f"squares_bf{b}")

@@ -87,7 +87,7 @@ def tile_nona_nn_kernel(tc, x, y, offs, out):
             )
 
         y_bf = held.tile([N, K], BF16, name="y_bf")
-        nc.scalar.copy(y_bf[:], y_f32[:])
+        nc.vector.tensor_copy(y_bf[:], y_f32[:])
 
         root = held.tile([N, N], F32, name="root")
         nc.scalar.activation(root[:], half[:], ACT.Abs_reciprocal_sqrt, bias=-SMALL, scale=0.5)

import concourse.mybir as mybir
from concourse.masks import make_identity

F32 = mybir.dt.float32
BF16 = mybir.dt.bfloat16
U16 = mybir.dt.uint16
ALU = mybir.AluOpType
ACT = mybir.ActivationFunctionType

P = 128
C, S, N, K = 512, 256, 128, 128
BLOCKS = C // P

BANK = 512
WARM_UPS = 4
KEEP_UPS = 2

FLOPS = 2 * N * N * C + 2 * N * N * K

SMALL = 2.0 ** -80
BIG = 2.0 ** 96


def tile_nona_nn_kernel(tc, x, y, offs, out):
    nc = tc.nc
    with (
        tc.tile_pool(name="held", bufs=1) as held,
        tc.psum_pool(name="psum", bufs=1) as psum,
    ):
        offsets = held.tile([P, N // 16], U16, name="offsets")
        x_rows = x.rearrange("(p b) s -> p (b s)", p=P)
        first = held.tile([P, S], F32, name="first")
        second = held.tile([P, S], F32, name="second")
        last_two = held.tile([P, 2 * S], F32, name="last_two")
        windows = [first[:], second[:], last_two[:, 0:S], last_two[:, S : 2 * S]]
        nc.sync.dma_start(first[:], x_rows[:, 0:S])
        nc.sync.dma_start(offsets[:], offs)
        nc.sync.dma_start(second[:], x_rows[:, S : 2 * S])
        nc.sync.dma_start(last_two[:], x_rows[:, 2 * S : 4 * S])
        y_f32 = held.tile([N, K], F32, name="y_f32")
        nc.sync.dma_start(y_f32[:], y)

        warm = held.tile([P, 1], F32, name="warm")
        nc.gpsimd.memset(warm[:], 1.0)
        nc.scalar.activation(warm[:], warm[:], ACT.Abs_reciprocal_sqrt)

        identity = held.tile([P, P], BF16, name="identity")
        make_identity(nc, identity[:])
        diagonal = held.tile([P, P], BF16, name="diagonal")
        nc.gpsimd.memset(diagonal[:], 0.0)
        nc.gpsimd.affine_select(
            out=diagonal[:],
            in_=diagonal[:],
            compare_op=ALU.not_equal,
            fill=-BIG / 2,
            base=0,
            pattern=[[-1, P]],
            channel_multiplier=1,
        )
        identity_f32 = held.tile([P, P], F32, name="identity_f32")
        nc.vector.tensor_copy(identity_f32[:], identity[:])
        minus_half = held.tile([P, P], BF16, name="minus_half")
        nc.vector.memset(minus_half[:], -0.5)

        filler = held.tile([P, BANK], BF16, name="filler")
        nc.vector.memset(filler[:], 0.0)
        unused = psum.tile([P, BANK], F32, name="unused")
        for warm_up in range(WARM_UPS):
            nc.tensor.matmul(unused[:], minus_half[:], filler[:], start=True, stop=True)

        half = psum.tile([N, N], F32, name="half")
        nc.tensor.matmul(half[:], identity[:], diagonal[:], start=True, stop=False)
        for b in range(BLOCKS):
            picked = held.tile([P, N], F32, name=f"picked{b}")
            nc.scalar.activation(picked[:], windows[b].indirect(offsets[:]), ACT.Copy)
            picked_bf = held.tile([P, N], BF16, name=f"picked_bf{b}")
            nc.vector.tensor_copy(picked_bf[:], picked[:])
            squares_bf = held.tile([P, N], BF16, name=f"squares_bf{b}")
            if b < BLOCKS - 1:
                nc.vector.tensor_tensor(squares_bf[:], picked[:], picked[:], ALU.mult)
            else:
                nc.scalar.activation(squares_bf[:], picked[:], ACT.Square)
            nc.tensor.matmul(half[:], picked_bf[:], picked_bf[:], start=False, stop=False)
            nc.tensor.matmul(half[:], minus_half[:], squares_bf[:], start=False, stop=False)
            nc.tensor.matmul(
                half[:], squares_bf[:], minus_half[:], start=False, stop=(b == BLOCKS - 1)
            )

        y_bf = held.tile([N, K], BF16, name="y_bf")
        nc.vector.tensor_copy(y_bf[:], y_f32[:])

        root = held.tile([N, N], F32, name="root")
        nc.scalar.activation(root[:], half[:], ACT.Abs_reciprocal_sqrt, bias=-SMALL, scale=0.5)
        minus_dist = held.tile([N, N], F32, name="minus_dist")
        nc.vector.scalar_tensor_tensor(minus_dist[:], half[:], 0.0, root[:], ALU.min, ALU.mult)
        nearest = held.tile([N, 1], BF16, name="nearest")
        nc.vector.tensor_reduce(
            nearest[:], minus_dist[:], axis=mybir.AxisListType.X, op=ALU.max, negate=True
        )

        exponents_t = psum.tile([N, N], F32, name="exponents_t")
        nc.tensor.matmul(exponents_t[:], identity_f32[:], minus_dist[:], start=True, stop=False)
        nc.tensor.matmul(
            exponents_t[:], nearest[:].to_broadcast([N, N]), identity[:], start=False, stop=True
        )

        for keep_up in range(KEEP_UPS):
            nc.tensor.matmul(
                unused[:], nearest[:].to_broadcast([N, N]), filler[:], start=True, stop=True
            )

        weights = held.tile([N, N], BF16, name="weights")
        total = held.tile([N, 1], F32, name="total")
        nc.scalar.activation(
            weights[:], minus_dist[:], ACT.Exp, bias=nearest[:], accum_out=total[:]
        )
        weights_t = held.tile([N, N], BF16, name="weights_t")
        nc.scalar.activation(weights_t[:], exponents_t[:], ACT.Exp)

        HALF = N // 2
        mixed_low_ps = psum.tile([K, HALF], F32, name="mixed_low_ps")
        mixed_high_ps = psum.tile([K, HALF], F32, name="mixed_high_ps")
        nc.tensor.matmul(mixed_low_ps[:], y_bf[:], weights_t[:, 0:HALF], start=True, stop=True)
        nc.tensor.matmul(mixed_high_ps[:], y_bf[:], weights_t[:, HALF:N], start=True, stop=True)

        inverse = held.tile([N, 1], F32, name="inverse")
        nc.vector.reciprocal(inverse[:], total[:])
        spread_ps = psum.tile([K, N], F32, name="spread_ps")
        nc.tensor.transpose(spread_ps[:], inverse[:].to_broadcast([N, K]), identity_f32[:])

        mixed = held.tile([K, N], F32, name="mixed")
        nc.vector.tensor_copy(mixed[:, 0:HALF], mixed_low_ps[:])
        nc.scalar.copy(mixed[:, HALF:N], mixed_high_ps[:])
        result = held.tile([K, N], F32, name="result")
        nc.vector.tensor_tensor(result[:], mixed[:], spread_ps[:], ALU.mult)
        nc.sync.dma_start(out, result[:])
